import numpy as np
import ml_dtypes


def mxq(x, axis, fmt="e4m3"):
    dtype, down = {"e4m3": (ml_dtypes.float8_e4m3fn, 7), "e5m2": (ml_dtypes.float8_e5m2, 14)}[fmt]
    v = np.moveaxis(np.asarray(x, np.float32).astype(ml_dtypes.bfloat16).astype(np.float64), axis, -1)
    blocks = v.reshape(v.shape[:-1] + (-1, 32))
    amax = np.abs(blocks).max(-1, keepdims=True)
    byte = np.maximum(np.where(amax > 0, np.frexp(amax)[1] - 1 + 127, 0) - down, 1)
    scale = np.exp2(byte - 127.0)
    codes = (blocks / scale).astype(np.float32).astype(dtype).astype(np.float64)
    return np.moveaxis((codes * scale).reshape(v.shape), -1, axis)


WIDE = False


def mx_kscale(k):
    if not WIDE:
        return np.ones(k)
    levels = np.array([10, -10, 5, -5, 0])
    a = np.random.permutation(np.resize(levels, k // 512 * 4)).reshape(k // 512, 4)
    idx = np.arange(k)
    return np.exp2(a[idx // 512, idx % 128 // 32])


BF16 = ml_dtypes.bfloat16


def bf(x):
    return np.asarray(x, np.float32).astype(BF16)


def f64(x):
    return np.asarray(x).astype(np.float64)


NQ, NK, QS, KS, F, DEG = 4096, 1024, 1024, 512, 512, 32
EPS = 1e-5
SLOPE = 0.01


def leaky(v):
    return np.where(v >= 0, v, SLOPE * v)


def setup_inputs():
    s, t = mx_kscale(QS), mx_kscale(F)
    return {"x": bf(np.random.standard_normal((NQ, QS)) * s),
            "w1": bf(np.random.standard_normal((QS, F)) / np.sqrt(QS) / s[:, None] * t),
            "b1": bf(np.random.standard_normal(F) * 0.5 * t),
            "w2": bf(np.random.standard_normal((F, F)) / np.sqrt(F) / t[:, None]),
            "b2": bf(np.random.standard_normal(F) * 0.5),
            "gamma": bf(1.0 + 0.1 * np.random.standard_normal(F)),
            "beta": bf(0.1 * np.random.standard_normal(F))}


def reference(x, w1, b1, w2, b2, gamma, beta):
    h = leaky((mxq(f64(x), 1, "e4m3") @ mxq(f64(w1), 0, "e4m3")) + f64(b1))
    h = leaky((mxq(h, 1, "e4m3") @ mxq(f64(w2), 0, "e4m3")) + f64(b2))
    mean = h.mean(axis=0)
    var = h.var(axis=0)
    return f64(gamma) * (h - mean) / np.sqrt(var + EPS) + f64(beta)

@@ -1,0 +1,331 @@
+from contextlib import ExitStack
+
+import concourse.masks as masks
+import concourse.mybir as mybir
+
+F32 = mybir.dt.float32
+BF16 = mybir.dt.bfloat16
+U32 = mybir.dt.uint32
+U8 = mybir.dt.uint8
+FP8X4 = mybir.dt.float8_e4m3fn_x4
+ALU = mybir.AluOpType
+ACT = mybir.ActivationFunctionType
+
+P = 128
+NQ, QS, F = 4096, 1024, 512
+CH = 512
+NCH = NQ // CH
+RT = CH // P
+NI = NQ // P
+FT = F // P
+EPS = 1e-5
+SLOPE = 0.01
+FLOPS = 2 * NQ * QS * F + 2 * NQ * F * F
+
+MANUAL = True
+GB = 2
+LAG = 2
+
+
+def tile_attention_prop_pa_t_kernel(tc, x, w1, b1, w2, b2, gamma, beta, out):
+    nc = tc.nc
+    with ExitStack() as ctx:
+        const = ctx.enter_context(tc.tile_pool(name="const", bufs=1))
+        wts = ctx.enter_context(tc.tile_pool(name="wts", bufs=1))
+        xin = ctx.enter_context(tc.tile_pool(name="xin", bufs=4))
+        xgp = ctx.enter_context(tc.tile_pool(name="xgp", bufs=2))
+        xqp = ctx.enter_context(tc.tile_pool(name="xqp", bufs=3))
+        v1p = ctx.enter_context(tc.tile_pool(name="v1p", bufs=2))
+        h1gp = ctx.enter_context(tc.tile_pool(name="h1gp", bufs=2))
+        h1qp = ctx.enter_context(tc.tile_pool(name="h1qp", bufs=1))
+        h2p = ctx.enter_context(tc.tile_pool(name="h2p", bufs=1))
+        s2p = ctx.enter_context(tc.tile_pool(name="s2p", bufs=4))
+        ostp = ctx.enter_context(tc.tile_pool(name="ostp", bufs=4))
+        pt = ctx.enter_context(tc.psum_pool(name="pt", bufs=4))
+        pm = ctx.enter_context(tc.psum_pool(name="pm", bufs=4))
+        if MANUAL:
+            ctx.enter_context(tc.manual_schedule())
+
+        x_v = x.rearrange("(p i) k -> p i k", i=NI)
+        out_v = out.rearrange("(p i) f -> p i f", i=NI)
+
+        b1t = const.tile([P, FT], BF16, name="b1t")
+        b2t = const.tile([P, FT], BF16, name="b2t")
+        gat = const.tile([P, FT], BF16, name="gat")
+        bet = const.tile([P, FT], BF16, name="bet")
+        nc.scalar.dma_start(out=b1t[:], in_=b1.rearrange("(p t) -> p t", t=FT))
+        with nc.allow_non_contiguous_dma(reason="512 values, one to a partition and feature tile"):
+            nc.scalar.dma_start(out=b2t[:], in_=b2.rearrange("(t p) -> p t", p=P))
+            nc.scalar.dma_start(out=gat[:], in_=gamma.rearrange("(t p) -> p t", p=P))
+            nc.scalar.dma_start(out=bet[:], in_=beta.rearrange("(t p) -> p t", p=P))
+
+        w1raw = wts.tile([P, 4096], BF16, name="w1raw")
+        w1_v = w1.rearrange("(a q e) c -> q a e c", a=4, q=P, e=2)
+        for g in range(2):
+            nc.sync.dma_start(
+                out=w1raw[:, 2048 * g : 2048 * (g + 1)].rearrange("p (a e c) -> p a e c", a=2, e=2),
+                in_=w1_v[:, 2 * g : 2 * g + 2],
+            )
+
+        xt_tiles = {}
+
+        def load_x(c):
+            xc = xin.tile([P, RT * QS], BF16, name="xc")
+            xt_tiles[c] = xc
+            if c == 0:
+                for i in range(RT):
+                    nc.sync.dma_start(out=xc[:, QS * i : QS * (i + 1)], in_=x_v[:, i, :])
+            else:
+                nc.sync.dma_start(
+                    out=xc[:].rearrange("p (i k) -> p i k", i=RT), in_=x_v[:, RT * c : RT * (c + 1), :]
+                )
+
+        load_x(0)
+        load_x(1)
+        w2raw = wts.tile([P, 2048], BF16, name="w2raw")
+        nc.sync.dma_start(
+            out=w2raw[:].rearrange("p (t c) -> p t c", t=4), in_=w2.rearrange("(p t) c -> p t c", t=4)
+        )
+        load_x(2)
+        load_x(3)
+
+        ident = const.tile([P, P], F32, name="ident")
+        masks.make_identity(nc, ident[:])
+        mhalf = const.tile([P, 1], F32, name="mhalf")
+        nc.gpsimd.memset(mhalf[:], -0.5)
+        b1f = const.tile([P, FT], F32, name="b1f")
+        b2f = const.tile([P, FT], F32, name="b2f")
+        b2s = const.tile([P, FT], F32, name="b2s")
+        gaf = const.tile([P, FT], F32, name="gaf")
+        bef = const.tile([P, FT], F32, name="bef")
+        nc.gpsimd.tensor_copy(out=b1f[:], in_=b1t[:])
+        nc.gpsimd.tensor_copy(out=b2f[:], in_=b2t[:])
+        nc.gpsimd.tensor_scalar(out=b2s[:], in0=b2t[:], scalar1=SLOPE, scalar2=0.0, op0=ALU.mult, op1=ALU.add)
+        nc.gpsimd.tensor_copy(out=gaf[:], in_=gat[:])
+        nc.gpsimd.tensor_copy(out=bef[:], in_=bet[:])
+
+        w1g = wts.tile([P, 4096], BF16, name="w1g", align_bytes=64)
+        w1q = wts.tile([P, 1024], U32, name="w1q", align_bytes=64)
+        w1s = wts.tile([P, 1024], U8, name="w1s", align_bytes=64)
+        for g in range(2):
+            nc.vector.tensor_copy(
+                out=w1g[:, 2048 * g : 2048 * (g + 1)].rearrange("p (t m j) -> p t m j", t=4, m=P, j=4),
+                in_=w1raw[:, 2048 * g : 2048 * (g + 1)].rearrange("p (j m t) -> p t m j", j=4, m=P, t=4),
+            )
+        for g in range(2):
+            nc.vector.quantize_mx(
+                out=w1q[:, 512 * g : 512 * (g + 1)].bitcast(FP8X4),
+                scales=w1s[:, 512 * g : 512 * (g + 1)],
+                in_=w1g[:, 2048 * g : 2048 * (g + 1)],
+            )
+        w2g = wts.tile([P, 2048], BF16, name="w2g", align_bytes=64)
+        w2q = wts.tile([P, 512], U32, name="w2q", align_bytes=64)
+        w2s = wts.tile([P, 512], U8, name="w2s", align_bytes=64)
+
+        def prep_w2():
+            nc.vector.tensor_copy(
+                out=w2g[:].rearrange("p (c t) -> p c t", t=4), in_=w2raw[:].rearrange("p (t c) -> p c t", t=4)
+            )
+            nc.vector.quantize_mx(out=w2q[:].bitcast(FP8X4), scales=w2s[:], in_=w2g[:])
+
+        xbanks = {}
+        xgs = {}
+        xqs = {}
+        m1banks = {}
+        v1s = {}
+        h1gs = {}
+        h1qs = {}
+        m2banks = {}
+        s2s = {}
+        h2s = {}
+        obanks = {}
+        stats = [const.tile([P, 6 * NCH], F32, name="stats%d" % t) for t in range(FT)]
+        coefs = {}
+
+        def t_x(c):
+            xw = xt_tiles[c][:].bitcast(F32)
+            for i in range(RT):
+                bank = pt.tile([P, 512], F32, name="ptb")
+                xbanks[(c, i)] = bank
+                for q in range(4):
+                    nc.tensor.transpose(
+                        bank[:, P * q : P * (q + 1)], xw[:, 512 * i + P * q : 512 * i + P * (q + 1)], ident[:]
+                    )
+
+        def xe(c):
+            xg = xgp.tile([P, 4096], BF16, name="xg", align_bytes=64)
+            xgs[c] = xg
+            xg32 = xg[:].bitcast(F32).rearrange("p (g r u) -> p g r u", g=2, r=CH, u=2)
+            for i in range(RT):
+                nc.scalar.copy(
+                    out=xg32[:, :, P * i : P * (i + 1), :],
+                    in_=xbanks[(c, i)][:].rearrange("p (g u r) -> p g r u", g=2, u=2, r=P),
+                )
+
+        def qx(c):
+            xq = xqp.tile([P, 1024], U32, name="xq", align_bytes=64)
+            xs = xqp.tile([P, 1024], U8, name="xs", align_bytes=64)
+            xqs[c] = (xq, xs)
+            nc.vector.quantize_mx(out=xq[:].bitcast(FP8X4), scales=xs[:], in_=xgs[c][:])
+
+        def m1(c):
+            xq, xs = xqs[c]
+            for t in range(FT):
+                bank = pm.tile([P, 512], F32, name="pmb")
+                m1banks[(c, t)] = bank
+                for g in range(2):
+                    lo = 512 * g + P * t
+                    nc.tensor.matmul_mx(
+                        out=bank[:],
+                        lhsT=w1q[:, lo : lo + P].bitcast(FP8X4),
+                        lhsT_scale=w1s[:, lo : lo + P],
+                        rhs=xq[:, 512 * g : 512 * (g + 1)].bitcast(FP8X4),
+                        rhs_scale=xs[:, 512 * g : 512 * (g + 1)],
+                        start=(g == 0),
+                        stop=(g == 1),
+                    )
+
+        def bias1(c):
+            v1 = v1p.tile([P, 2048], F32, name="v1")
+            v1s[c] = v1
+            for t in range(FT):
+                nc.scalar.activation(
+                    out=v1[:, 512 * t : 512 * (t + 1)],
+                    in_=m1banks[(c, t)][:],
+                    func=ACT.Identity,
+                    bias=b1f[:, t : t + 1],
+                    scale=1.0,
+                )
+
+        def st1(c):
+            h1g = h1gp.tile([P, 2048], BF16, name="h1g", align_bytes=64)
+            h1gs[c] = h1g
+            v = v1s[c][:].rearrange("p (t w) -> p w t", t=FT)
+            nc.vector.scalar_tensor_tensor(
+                out=h1g[:].rearrange("p (w t) -> p w t", t=FT), in0=v, scalar=SLOPE, in1=v, op0=ALU.mult, op1=ALU.max
+            )
+
+        def qh(c):
+            hq = h1qp.tile([P, 512], U32, name="h1q%d" % c, align_bytes=64)
+            hs = h1qp.tile([P, 512], U8, name="h1s%d" % c, align_bytes=64)
+            h1qs[c] = (hq, hs)
+            nc.vector.quantize_mx(out=hq[:].bitcast(FP8X4), scales=hs[:], in_=h1gs[c][:])
+
+        def m2(c, t):
+            hq, hs = h1qs[c]
+            bank = pm.tile([P, 512], F32, name="pmb")
+            m2banks[(c, t)] = bank
+            nc.tensor.matmul_mx(
+                out=bank[:],
+                lhsT=w2q[:, P * t : P * (t + 1)].bitcast(FP8X4),
+                lhsT_scale=w2s[:, P * t : P * (t + 1)],
+                rhs=hq[:].bitcast(FP8X4),
+                rhs_scale=hs[:],
+                start=True,
+                stop=True,
+            )
+
+        def s2(c, t):
+            s = s2p.tile([P, 512], F32, name="s2")
+            s2s[(c, t)] = s
+            nc.scalar.activation(
+                out=s[:], in_=m2banks[(c, t)][:], func=ACT.Identity, bias=b2s[:, t : t + 1], scale=SLOPE
+            )
+
+        def st2(c, t):
+            h2 = h2p.tile([P, 512], F32, name="h2_%d_%d" % (t, c))
+            h2s[(c, t)] = h2
+            nc.vector.scalar_tensor_tensor(
+                out=h2[:],
+                in0=m2banks[(c, t)][:],
+                scalar=b2f[:, t : t + 1],
+                in1=s2s[(c, t)][:],
+                op0=ALU.add,
+                op1=ALU.max,
+            )
+            nc.vector.bn_stats(out=stats[t][:, 6 * c : 6 * (c + 1)], in_=h2[:])
+
+        def agg(t):
+            mv = const.tile([P, 2], F32, name="mv%d" % t)
+            ve = const.tile([P, 1], F32, name="ve%d" % t)
+            rstd = const.tile([P, 1], F32, name="rstd%d" % t)
+            ca = const.tile([P, 1], F32, name="ca%d" % t)
+            ma = const.tile([P, 1], F32, name="ma%d" % t)
+            cb = const.tile([P, 1], F32, name="cb%d" % t)
+            coefs[t] = (ca, cb)
+            nc.vector.bn_aggr(out=mv[:], in_=stats[t][:])
+            nc.gpsimd.tensor_scalar(out=ve[:], in0=mv[:, 1:2], scalar1=1.0, scalar2=EPS, op0=ALU.mult, op1=ALU.add)
+            nc.gpsimd.tensor_tensor(out=rstd[:], in0=ve[:], in1=mhalf[:], op=ALU.pow)
+            nc.gpsimd.tensor_tensor(out=ca[:], in0=rstd[:], in1=gaf[:, t : t + 1], op=ALU.mult)
+            nc.gpsimd.tensor_tensor(out=ma[:], in0=mv[:, 0:1], in1=ca[:], op=ALU.mult)
+            nc.gpsimd.tensor_tensor(out=cb[:], in0=bef[:, t : t + 1], in1=ma[:], op=ALU.subtract)
+
+        def norm(c, t, eng):
+            ca, cb = coefs[t]
+            h2 = h2s[(c, t)]
+            eng.tensor_scalar(out=h2[:], in0=h2[:], scalar1=ca[:, 0:1], scalar2=cb[:, 0:1], op0=ALU.mult, op1=ALU.add)
+
+        def t_o(c, t):
+            bank = pt.tile([P, 512], F32, name="ptb")
+            obanks[(c, t)] = bank
+            h2 = h2s[(c, t)]
+            for i in range(RT):
+                nc.tensor.transpose(bank[:, P * i : P * (i + 1)], h2[:, P * i : P * (i + 1)], ident[:])
+
+        def ex(c, t):
+            ost = ostp.tile([P, 512], F32, name="ost")
+            nc.scalar.copy(out=ost[:], in_=obanks[(c, t)][:])
+            nc.sync.dma_start(
+                out=out_v[:, RT * c : RT * (c + 1), P * t : P * (t + 1)], in_=ost[:].rearrange("p (i f) -> p i f", i=RT)
+            )
+
+        for n in range(-2, NCH + 1):
+            if 0 <= n - 1 < NCH:
+                m2(n - 1, 0)
+            if 0 <= n < NCH:
+                bias1(n)
+            if n + 2 < NCH:
+                t_x(n + 2)
+                if n + 6 < NCH:
+                    load_x(n + 6)
+            if 0 <= n < NCH:
+                st1(n)
+            if 0 <= n - 1 < NCH:
+                s2(n - 1, 0)
+                st2(n - 1, 0)
+            if n == 0:
+                prep_w2()
+            if 0 <= n < NCH:
+                qh(n)
+            if 0 <= n + 1 < NCH:
+                m1(n + 1)
+            if n + 2 < NCH:
+                xe(n + 2)
+                qx(n + 2)
+        agg(0)
+        for c in range(NCH):
+            norm(c, 0, nc.gpsimd)
+
+        lu = [(c, t) for t in range(1, FT) for c in range(NCH)]
+        pu = [(c, t) for t in range(0, FT - 1) for c in range(NCH)]
+        for k in range(0, len(lu) + LAG, GB):
+            la = [lu[j] for j in range(k, k + GB) if j < len(lu)]
+            pa = [pu[j] for j in range(k - LAG, k - LAG + GB) if 0 <= j < len(pu)]
+            for c, t in la:
+                m2(c, t)
+            for c, t in pa:
+                t_o(c, t)
+            for c, t in la:
+                s2(c, t)
+            for c, t in la:
+                st2(c, t)
+            for c, t in pa:
+                ex(c, t)
+            for c, t in la:
+                if c == NCH - 1:
+                    agg(t)
+                    for cc in range(NCH):
+                        norm(cc, t, nc.gpsimd if t < FT - 1 else nc.vector)
+        for c in range(NCH):
+            t_o(c, FT - 1)
+            ex(c, FT - 1)

@@ -22,7 +22,7 @@ EPS = 1e-5
 SLOPE = 0.01
 FLOPS = 2 * NQ * QS * F + 2 * NQ * F * F
 
-MANUAL = True
+MANUAL = False
 GB = 2
 LAG = 2
 

@@ -22,9 +22,10 @@ EPS = 1e-5
 SLOPE = 0.01
 FLOPS = 2 * NQ * QS * F + 2 * NQ * F * F
 
-MANUAL = False
+MANUAL = True
 GB = 2
-LAG = 2
+PLAG = 2
+EXTRA = {6: 1, 7: 1}
 
 
 def tile_attention_prop_pa_t_kernel(tc, x, w1, b1, w2, b2, gamma, beta, out):
@@ -107,17 +108,20 @@ def tile_attention_prop_pa_t_kernel(tc, x, w1, b1, w2, b2, gamma, beta, out):
         w1g = wts.tile([P, 4096], BF16, name="w1g", align_bytes=64)
         w1q = wts.tile([P, 1024], U32, name="w1q", align_bytes=64)
         w1s = wts.tile([P, 1024], U8, name="w1s", align_bytes=64)
-        for g in range(2):
-            nc.vector.tensor_copy(
-                out=w1g[:, 2048 * g : 2048 * (g + 1)].rearrange("p (t m j) -> p t m j", t=4, m=P, j=4),
-                in_=w1raw[:, 2048 * g : 2048 * (g + 1)].rearrange("p (j m t) -> p t m j", j=4, m=P, t=4),
-            )
-        for g in range(2):
-            nc.vector.quantize_mx(
-                out=w1q[:, 512 * g : 512 * (g + 1)].bitcast(FP8X4),
-                scales=w1s[:, 512 * g : 512 * (g + 1)],
-                in_=w1g[:, 2048 * g : 2048 * (g + 1)],
-            )
+
+        def prep_w1():
+            for g in range(2):
+                nc.vector.tensor_copy(
+                    out=w1g[:, 2048 * g : 2048 * (g + 1)].rearrange("p (t m j) -> p t m j", t=4, m=P, j=4),
+                    in_=w1raw[:, 2048 * g : 2048 * (g + 1)].rearrange("p (j m t) -> p t m j", j=4, m=P, t=4),
+                )
+            for g in range(2):
+                nc.vector.quantize_mx(
+                    out=w1q[:, 512 * g : 512 * (g + 1)].bitcast(FP8X4),
+                    scales=w1s[:, 512 * g : 512 * (g + 1)],
+                    in_=w1g[:, 2048 * g : 2048 * (g + 1)],
+                )
+
         w2g = wts.tile([P, 2048], BF16, name="w2g", align_bytes=64)
         w2q = wts.tile([P, 512], U32, name="w2q", align_bytes=64)
         w2s = wts.tile([P, 512], U8, name="w2s", align_bytes=64)
@@ -151,6 +155,8 @@ def tile_attention_prop_pa_t_kernel(tc, x, w1, b1, w2, b2, gamma, beta, out):
                     nc.tensor.transpose(
                         bank[:, P * q : P * (q + 1)], xw[:, 512 * i + P * q : 512 * i + P * (q + 1)], ident[:]
                     )
+            if c + 4 < NCH:
+                load_x(c + 4)
 
         def xe(c):
             xg = xgp.tile([P, 4096], BF16, name="xg", align_bytes=64)
@@ -225,24 +231,34 @@ def tile_attention_prop_pa_t_kernel(tc, x, w1, b1, w2, b2, gamma, beta, out):
                 stop=True,
             )
 
-        def s2(c, t):
+        def s2(c, t, whole):
             s = s2p.tile([P, 512], F32, name="s2")
             s2s[(c, t)] = s
-            nc.scalar.activation(
-                out=s[:], in_=m2banks[(c, t)][:], func=ACT.Identity, bias=b2s[:, t : t + 1], scale=SLOPE
-            )
+            if whole:
+                nc.scalar.activation(
+                    out=s[:], in_=m2banks[(c, t)][:], func=ACT.Identity, bias=b2f[:, t : t + 1], scale=1.0
+                )
+            else:
+                nc.scalar.activation(
+                    out=s[:], in_=m2banks[(c, t)][:], func=ACT.Identity, bias=b2s[:, t : t + 1], scale=SLOPE
+                )
 
-        def st2(c, t):
+        def st2(c, t, whole):
             h2 = h2p.tile([P, 512], F32, name="h2_%d_%d" % (t, c))
             h2s[(c, t)] = h2
-            nc.vector.scalar_tensor_tensor(
-                out=h2[:],
-                in0=m2banks[(c, t)][:],
-                scalar=b2f[:, t : t + 1],
-                in1=s2s[(c, t)][:],
-                op0=ALU.add,
-                op1=ALU.max,
-            )
+            if whole:
+                nc.vector.scalar_tensor_tensor(
+                    out=h2[:], in0=s2s[(c, t)][:], scalar=SLOPE, in1=s2s[(c, t)][:], op0=ALU.mult, op1=ALU.max
+                )
+            else:
+                nc.vector.scalar_tensor_tensor(
+                    out=h2[:],
+                    in0=m2banks[(c, t)][:],
+                    scalar=b2f[:, t : t + 1],
+                    in1=s2s[(c, t)][:],
+                    op0=ALU.add,
+                    op1=ALU.max,
+                )
             nc.vector.bn_stats(out=stats[t][:, 6 * c : 6 * (c + 1)], in_=h2[:])
 
         def agg(t):
@@ -279,53 +295,81 @@ def tile_attention_prop_pa_t_kernel(tc, x, w1, b1, w2, b2, gamma, beta, out):
                 out=out_v[:, RT * c : RT * (c + 1), P * t : P * (t + 1)], in_=ost[:].rearrange("p (i f) -> p i f", i=RT)
             )
 
-        for n in range(-2, NCH + 1):
-            if 0 <= n - 1 < NCH:
-                m2(n - 1, 0)
-            if 0 <= n < NCH:
-                bias1(n)
-            if n + 2 < NCH:
-                t_x(n + 2)
-                if n + 6 < NCH:
-                    load_x(n + 6)
-            if 0 <= n < NCH:
-                st1(n)
-            if 0 <= n - 1 < NCH:
-                s2(n - 1, 0)
-                st2(n - 1, 0)
-            if n == 0:
-                prep_w2()
-            if 0 <= n < NCH:
-                qh(n)
-            if 0 <= n + 1 < NCH:
-                m1(n + 1)
-            if n + 2 < NCH:
-                xe(n + 2)
-                qx(n + 2)
-        agg(0)
-        for c in range(NCH):
-            norm(c, 0, nc.gpsimd)
+        units = [(c, t) for t in range(FT) for c in range(NCH)]
+        pos = {"m": 0, "s": 0, "v": 0, "p": 0, "e": 0, "step": 0}
+        agg_step = {}
 
-        lu = [(c, t) for t in range(1, FT) for c in range(NCH)]
-        pu = [(c, t) for t in range(0, FT - 1) for c in range(NCH)]
-        for k in range(0, len(lu) + LAG, GB):
-            la = [lu[j] for j in range(k, k + GB) if j < len(lu)]
-            pa = [pu[j] for j in range(k - LAG, k - LAG + GB) if 0 <= j < len(pu)]
-            for c, t in la:
-                m2(c, t)
-            for c, t in pa:
-                t_o(c, t)
-            for c, t in la:
-                s2(c, t)
-            for c, t in la:
-                st2(c, t)
-            for c, t in pa:
-                ex(c, t)
-            for c, t in la:
+        whole_of = {}
+
+        def v_units():
+            while pos["v"] < pos["s"]:
+                c, t = units[pos["v"]]
+                st2(c, t, whole_of[(c, t)])
+                pos["v"] += 1
                 if c == NCH - 1:
                     agg(t)
+                    agg_step[t] = pos["step"]
                     for cc in range(NCH):
                         norm(cc, t, nc.gpsimd if t < FT - 1 else nc.vector)
-        for c in range(NCH):
-            t_o(c, FT - 1)
-            ex(c, FT - 1)
+
+        t_x(0)
+        xe(0)
+        prep_w1()
+        t_x(1)
+        qx(0)
+        xe(1)
+        m1(0)
+        t_x(2)
+        bias1(0)
+        qx(1)
+        prep_w2()
+        xe(2)
+        for n in range(NCH):
+            pos["step"] += 1
+            if n + 1 < NCH:
+                m1(n + 1)
+            if n + 3 < NCH:
+                t_x(n + 3)
+            mu = []
+            for j in range((1 if n >= 1 else 0) + EXTRA.get(n, 0)):
+                if units[pos["m"]][0] <= n - 1:
+                    mu.append(units[pos["m"]])
+                    pos["m"] += 1
+            for c, t in mu:
+                m2(c, t)
+            st1(n)
+            v_units()
+            qh(n)
+            if n + 2 < NCH:
+                qx(n + 2)
+            if n + 1 < NCH:
+                bias1(n + 1)
+            if n + 3 < NCH:
+                xe(n + 3)
+            for c, t in mu:
+                s2(c, t, True)
+                whole_of[(c, t)] = True
+                pos["s"] += 1
+        while pos["v"] < len(units) or pos["e"] < len(units):
+            pos["step"] += 1
+            mu = units[pos["m"] : pos["m"] + GB]
+            pos["m"] += len(mu)
+            for c, t in mu:
+                m2(c, t)
+            pa = []
+            for j in range(GB):
+                if pos["p"] < len(units):
+                    u = units[pos["p"]]
+                    if u[1] in agg_step and pos["step"] - agg_step[u[1]] >= PLAG:
+                        pa.append(u)
+                        pos["p"] += 1
+            for c, t in pa:
+                t_o(c, t)
+            v_units()
+            for c, t in mu:
+                s2(c, t, False)
+                whole_of[(c, t)] = False
+                pos["s"] += 1
+            for c, t in pa:
+                ex(c, t)
+                pos["e"] += 1

@@ -22,7 +22,7 @@ EPS = 1e-5
 SLOPE = 0.01
 FLOPS = 2 * NQ * QS * F + 2 * NQ * F * F
 
-MANUAL = True
+MANUAL = False
 GB = 2
 PLAG = 2
 EXTRA = {6: 1, 7: 1}

@@ -40,8 +40,8 @@ def tile_attention_prop_pa_t_kernel(tc, x, w1, b1, w2, b2, gamma, beta, out):
         h1gp = ctx.enter_context(tc.tile_pool(name="h1gp", bufs=2))
         h1qp = ctx.enter_context(tc.tile_pool(name="h1qp", bufs=1))
         h2p = ctx.enter_context(tc.tile_pool(name="h2p", bufs=1))
-        s2p = ctx.enter_context(tc.tile_pool(name="s2p", bufs=4))
-        ostp = ctx.enter_context(tc.tile_pool(name="ostp", bufs=4))
+        s2p = ctx.enter_context(tc.tile_pool(name="s2p", bufs=6))
+        ostp = ctx.enter_context(tc.tile_pool(name="ostp", bufs=6))
         pt = ctx.enter_context(tc.psum_pool(name="pt", bufs=4))
         pm = ctx.enter_context(tc.psum_pool(name="pm", bufs=4))
         if MANUAL:
@@ -54,15 +54,11 @@ def tile_attention_prop_pa_t_kernel(tc, x, w1, b1, w2, b2, gamma, beta, out):
         b2t = const.tile([P, FT], BF16, name="b2t")
         gat = const.tile([P, FT], BF16, name="gat")
         bet = const.tile([P, FT], BF16, name="bet")
-        nc.scalar.dma_start(out=b1t[:], in_=b1.rearrange("(p t) -> p t", t=FT))
-        with nc.allow_non_contiguous_dma(reason="512 values, one to a partition and feature tile"):
-            nc.scalar.dma_start(out=b2t[:], in_=b2.rearrange("(t p) -> p t", p=P))
-            nc.scalar.dma_start(out=gat[:], in_=gamma.rearrange("(t p) -> p t", p=P))
-            nc.scalar.dma_start(out=bet[:], in_=beta.rearrange("(t p) -> p t", p=P))
 
         w1raw = wts.tile([P, 4096], BF16, name="w1raw")
         w1_v = w1.rearrange("(a q e) c -> q a e c", a=4, q=P, e=2)
-        for g in range(2):
+
+        def load_w1(g):
             nc.sync.dma_start(
                 out=w1raw[:, 2048 * g : 2048 * (g + 1)].rearrange("p (a e c) -> p a e c", a=2, e=2),
                 in_=w1_v[:, 2 * g : 2 * g + 2],
@@ -76,6 +72,8 @@ def tile_attention_prop_pa_t_kernel(tc, x, w1, b1, w2, b2, gamma, beta, out):
             if c == 0:
                 for i in range(RT):
                     nc.sync.dma_start(out=xc[:, QS * i : QS * (i + 1)], in_=x_v[:, i, :])
+                    if i % 2 == 1:
+                        load_w1(i // 2)
             else:
                 nc.sync.dma_start(
                     out=xc[:].rearrange("p (i k) -> p i k", i=RT), in_=x_v[:, RT * c : RT * (c + 1), :]
@@ -87,7 +85,12 @@ def tile_attention_prop_pa_t_kernel(tc, x, w1, b1, w2, b2, gamma, beta, out):
         nc.sync.dma_start(
             out=w2raw[:].rearrange("p (t c) -> p t c", t=4), in_=w2.rearrange("(p t) c -> p t c", t=4)
         )
+        nc.sync.dma_start(out=b1t[:], in_=b1.rearrange("(p t) -> p t", t=FT))
         load_x(2)
+        with nc.allow_non_contiguous_dma(reason="512 values, one to a partition and feature tile"):
+            nc.sync.dma_start(out=b2t[:], in_=b2.rearrange("(t p) -> p t", p=P))
+            nc.sync.dma_start(out=gat[:], in_=gamma.rearrange("(t p) -> p t", p=P))
+            nc.sync.dma_start(out=bet[:], in_=beta.rearrange("(t p) -> p t", p=P))
         load_x(3)
 
         ident = const.tile([P, P], F32, name="ident")
@@ -290,7 +293,10 @@ def tile_attention_prop_pa_t_kernel(tc, x, w1, b1, w2, b2, gamma, beta, out):
 
         def ex(c, t):
             ost = ostp.tile([P, 512], F32, name="ost")
-            nc.scalar.copy(out=ost[:], in_=obanks[(c, t)][:])
+            if t == FT - 1 and c % 2 == 1:
+                nc.vector.tensor_copy(out=ost[:], in_=obanks[(c, t)][:])
+            else:
+                nc.scalar.copy(out=ost[:], in_=obanks[(c, t)][:])
             nc.sync.dma_start(
                 out=out_v[:, RT * c : RT * (c + 1), P * t : P * (t + 1)], in_=ost[:].rearrange("p (i f) -> p i f", i=RT)
             )

@@ -373,8 +373,8 @@ def tile_attention_prop_pa_t_kernel(tc, x, w1, b1, w2, b2, gamma, beta, out):
                 t_o(c, t)
             v_units()
             for c, t in mu:
-                s2(c, t, False)
-                whole_of[(c, t)] = False
+                s2(c, t, True)
+                whole_of[(c, t)] = True
                 pos["s"] += 1
             for c, t in pa:
                 ex(c, t)

@@ -262,7 +262,9 @@ def tile_attention_prop_pa_t_kernel(tc, x, w1, b1, w2, b2, gamma, beta, out):
                     op0=ALU.add,
                     op1=ALU.max,
                 )
-            nc.vector.bn_stats(out=stats[t][:, 6 * c : 6 * (c + 1)], in_=h2[:])
+
+        def bn(c, t):
+            nc.vector.bn_stats(out=stats[t][:, 6 * c : 6 * (c + 1)], in_=h2s[(c, t)][:])
 
         def agg(t):
             mv = const.tile([P, 2], F32, name="mv%d" % t)
@@ -307,16 +309,23 @@ def tile_attention_prop_pa_t_kernel(tc, x, w1, b1, w2, b2, gamma, beta, out):
 
         whole_of = {}
 
+        def stats_of(c, t):
+            bn(c, t)
+            if c == NCH - 1:
+                agg(t)
+                agg_step[t] = pos["step"]
+                for cc in range(NCH):
+                    norm(cc, t, nc.gpsimd if t < FT - 1 else nc.vector)
+
         def v_units():
             while pos["v"] < pos["s"]:
                 c, t = units[pos["v"]]
                 st2(c, t, whole_of[(c, t)])
+                if pos["v"] > 0:
+                    stats_of(units[pos["v"] - 1][0], units[pos["v"] - 1][1])
                 pos["v"] += 1
-                if c == NCH - 1:
-                    agg(t)
-                    agg_step[t] = pos["step"]
-                    for cc in range(NCH):
-                        norm(cc, t, nc.gpsimd if t < FT - 1 else nc.vector)
+                if pos["v"] == len(units):
+                    stats_of(c, t)
 
         t_x(0)
         xe(0)
@@ -373,8 +382,8 @@ def tile_attention_prop_pa_t_kernel(tc, x, w1, b1, w2, b2, gamma, beta, out):
                 t_o(c, t)
             v_units()
             for c, t in mu:
-                s2(c, t, True)
-                whole_of[(c, t)] = True
+                s2(c, t, False)
+                whole_of[(c, t)] = False
                 pos["s"] += 1
             for c, t in pa:
                 ex(c, t)

from contextlib import ExitStack

import concourse.masks as masks
import concourse.mybir as mybir

F32 = mybir.dt.float32
BF16 = mybir.dt.bfloat16
U32 = mybir.dt.uint32
U8 = mybir.dt.uint8
FP8X4 = mybir.dt.float8_e4m3fn_x4
ALU = mybir.AluOpType
ACT = mybir.ActivationFunctionType

P = 128
NQ, QS, F = 4096, 1024, 512
CH = 512
NCH = NQ // CH
RT = CH // P
NI = NQ // P
FT = F // P
EPS = 1e-5
SLOPE = 0.01
FLOPS = 2 * NQ * QS * F + 2 * NQ * F * F

MANUAL = False
GB = 2
PLAG = 2
EXTRA = {6: 1, 7: 1}


def tile_attention_prop_pa_t_kernel(tc, x, w1, b1, w2, b2, gamma, beta, out):
    nc = tc.nc
    with ExitStack() as ctx:
        const = ctx.enter_context(tc.tile_pool(name="const", bufs=1))
        wts = ctx.enter_context(tc.tile_pool(name="wts", bufs=1))
        xin = ctx.enter_context(tc.tile_pool(name="xin", bufs=4))
        xgp = ctx.enter_context(tc.tile_pool(name="xgp", bufs=2))
        xqp = ctx.enter_context(tc.tile_pool(name="xqp", bufs=3))
        v1p = ctx.enter_context(tc.tile_pool(name="v1p", bufs=2))
        h1gp = ctx.enter_context(tc.tile_pool(name="h1gp", bufs=2))
        h1qp = ctx.enter_context(tc.tile_pool(name="h1qp", bufs=1))
        h2p = ctx.enter_context(tc.tile_pool(name="h2p", bufs=1))
        s2p = ctx.enter_context(tc.tile_pool(name="s2p", bufs=6))
        ostp = ctx.enter_context(tc.tile_pool(name="ostp", bufs=6))
        pt = ctx.enter_context(tc.psum_pool(name="pt", bufs=4))
        pm = ctx.enter_context(tc.psum_pool(name="pm", bufs=4))
        if MANUAL:
            ctx.enter_context(tc.manual_schedule())

        x_v = x.rearrange("(p i) k -> p i k", i=NI)
        out_v = out.rearrange("(p i) f -> p i f", i=NI)

        b1t = const.tile([P, FT], BF16, name="b1t")
        b2t = const.tile([P, FT], BF16, name="b2t")
        gat = const.tile([P, FT], BF16, name="gat")
        bet = const.tile([P, FT], BF16, name="bet")

        w1raw = wts.tile([P, 4096], BF16, name="w1raw")
        w1_v = w1.rearrange("(a q e) c -> q a e c", a=4, q=P, e=2)

        def load_w1(g):
            nc.sync.dma_start(
                out=w1raw[:, 2048 * g : 2048 * (g + 1)].rearrange("p (a e c) -> p a e c", a=2, e=2),
                in_=w1_v[:, 2 * g : 2 * g + 2],
            )

        xt_tiles = {}

        def load_x(c):
            xc = xin.tile([P, RT * QS], BF16, name="xc")
            xt_tiles[c] = xc
            if c == 0:
                for i in range(RT):
                    nc.sync.dma_start(out=xc[:, QS * i : QS * (i + 1)], in_=x_v[:, i, :])
                    if i % 2 == 1:
                        load_w1(i // 2)
            else:
                nc.sync.dma_start(
                    out=xc[:].rearrange("p (i k) -> p i k", i=RT), in_=x_v[:, RT * c : RT * (c + 1), :]
                )

        load_x(0)
        load_x(1)
        w2raw = wts.tile([P, 2048], BF16, name="w2raw")
        nc.sync.dma_start(
            out=w2raw[:].rearrange("p (t c) -> p t c", t=4), in_=w2.rearrange("(p t) c -> p t c", t=4)
        )
        nc.sync.dma_start(out=b1t[:], in_=b1.rearrange("(p t) -> p t", t=FT))
        load_x(2)
        with nc.allow_non_contiguous_dma(reason="512 values, one to a partition and feature tile"):
            nc.sync.dma_start(out=b2t[:], in_=b2.rearrange("(t p) -> p t", p=P))
            nc.sync.dma_start(out=gat[:], in_=gamma.rearrange("(t p) -> p t", p=P))
            nc.sync.dma_start(out=bet[:], in_=beta.rearrange("(t p) -> p t", p=P))
        load_x(3)

        ident = const.tile([P, P], F32, name="ident")
        masks.make_identity(nc, ident[:])
        mhalf = const.tile([P, 1], F32, name="mhalf")
        nc.gpsimd.memset(mhalf[:], -0.5)
        b1f = const.tile([P, FT], F32, name="b1f")
        b2f = const.tile([P, FT], F32, name="b2f")
        b2s = const.tile([P, FT], F32, name="b2s")
        gaf = const.tile([P, FT], F32, name="gaf")
        bef = const.tile([P, FT], F32, name="bef")
        nc.gpsimd.tensor_copy(out=b1f[:], in_=b1t[:])
        nc.gpsimd.tensor_copy(out=b2f[:], in_=b2t[:])
        nc.gpsimd.tensor_scalar(out=b2s[:], in0=b2t[:], scalar1=SLOPE, scalar2=0.0, op0=ALU.mult, op1=ALU.add)
        nc.gpsimd.tensor_copy(out=gaf[:], in_=gat[:])
        nc.gpsimd.tensor_copy(out=bef[:], in_=bet[:])

        w1g = wts.tile([P, 4096], BF16, name="w1g", align_bytes=64)
        w1q = wts.tile([P, 1024], U32, name="w1q", align_bytes=64)
        w1s = wts.tile([P, 1024], U8, name="w1s", align_bytes=64)

        def prep_w1():
            for g in range(2):
                nc.vector.tensor_copy(
                    out=w1g[:, 2048 * g : 2048 * (g + 1)].rearrange("p (t m j) -> p t m j", t=4, m=P, j=4),
                    in_=w1raw[:, 2048 * g : 2048 * (g + 1)].rearrange("p (j m t) -> p t m j", j=4, m=P, t=4),
                )
            for g in range(2):
                nc.vector.quantize_mx(
                    out=w1q[:, 512 * g : 512 * (g + 1)].bitcast(FP8X4),
                    scales=w1s[:, 512 * g : 512 * (g + 1)],
                    in_=w1g[:, 2048 * g : 2048 * (g + 1)],
                )

        w2g = wts.tile([P, 2048], BF16, name="w2g", align_bytes=64)
        w2q = wts.tile([P, 512], U32, name="w2q", align_bytes=64)
        w2s = wts.tile([P, 512], U8, name="w2s", align_bytes=64)

        def prep_w2():
            nc.vector.tensor_copy(
                out=w2g[:].rearrange("p (c t) -> p c t", t=4), in_=w2raw[:].rearrange("p (t c) -> p c t", t=4)
            )
            nc.vector.quantize_mx(out=w2q[:].bitcast(FP8X4), scales=w2s[:], in_=w2g[:])

        xbanks = {}
        xgs = {}
        xqs = {}
        m1banks = {}
        v1s = {}
        h1gs = {}
        h1qs = {}
        m2banks = {}
        s2s = {}
        h2s = {}
        obanks = {}
        stats = [const.tile([P, 6 * NCH], F32, name="stats%d" % t) for t in range(FT)]
        coefs = {}

        def t_x(c):
            xw = xt_tiles[c][:].bitcast(F32)
            for i in range(RT):
                bank = pt.tile([P, 512], F32, name="ptb")
                xbanks[(c, i)] = bank
                for q in range(4):
                    nc.tensor.transpose(
                        bank[:, P * q : P * (q + 1)], xw[:, 512 * i + P * q : 512 * i + P * (q + 1)], ident[:]
                    )
            if c + 4 < NCH:
                load_x(c + 4)

        def xe(c):
            xg = xgp.tile([P, 4096], BF16, name="xg", align_bytes=64)
            xgs[c] = xg
            xg32 = xg[:].bitcast(F32).rearrange("p (g r u) -> p g r u", g=2, r=CH, u=2)
            for i in range(RT):
                nc.scalar.copy(
                    out=xg32[:, :, P * i : P * (i + 1), :],
                    in_=xbanks[(c, i)][:].rearrange("p (g u r) -> p g r u", g=2, u=2, r=P),
                )

        def qx(c):
            xq = xqp.tile([P, 1024], U32, name="xq", align_bytes=64)
            xs = xqp.tile([P, 1024], U8, name="xs", align_bytes=64)
            xqs[c] = (xq, xs)
            nc.vector.quantize_mx(out=xq[:].bitcast(FP8X4), scales=xs[:], in_=xgs[c][:])

        def m1(c):
            xq, xs = xqs[c]
            for t in range(FT):
                bank = pm.tile([P, 512], F32, name="pmb")
                m1banks[(c, t)] = bank
                for g in range(2):
                    lo = 512 * g + P * t
                    nc.tensor.matmul_mx(
                        out=bank[:],
                        lhsT=w1q[:, lo : lo + P].bitcast(FP8X4),
                        lhsT_scale=w1s[:, lo : lo + P],
                        rhs=xq[:, 512 * g : 512 * (g + 1)].bitcast(FP8X4),
                        rhs_scale=xs[:, 512 * g : 512 * (g + 1)],
                        start=(g == 0),
                        stop=(g == 1),
                    )

        def bias1(c):
            v1 = v1p.tile([P, 2048], F32, name="v1")
            v1s[c] = v1
            for t in range(FT):
                nc.scalar.activation(
                    out=v1[:, 512 * t : 512 * (t + 1)],
                    in_=m1banks[(c, t)][:],
                    func=ACT.Identity,
                    bias=b1f[:, t : t + 1],
                    scale=1.0,
                )

        def st1(c):
            h1g = h1gp.tile([P, 2048], BF16, name="h1g", align_bytes=64)
            h1gs[c] = h1g
            v = v1s[c][:].rearrange("p (t w) -> p w t", t=FT)
            nc.vector.scalar_tensor_tensor(
                out=h1g[:].rearrange("p (w t) -> p w t", t=FT), in0=v, scalar=SLOPE, in1=v, op0=ALU.mult, op1=ALU.max
            )

        def qh(c):
            hq = h1qp.tile([P, 512], U32, name="h1q%d" % c, align_bytes=64)
            hs = h1qp.tile([P, 512], U8, name="h1s%d" % c, align_bytes=64)
            h1qs[c] = (hq, hs)
            nc.vector.quantize_mx(out=hq[:].bitcast(FP8X4), scales=hs[:], in_=h1gs[c][:])

        def m2(c, t):
            hq, hs = h1qs[c]
            bank = pm.tile([P, 512], F32, name="pmb")
            m2banks[(c, t)] = bank
            nc.tensor.matmul_mx(
                out=bank[:],
                lhsT=w2q[:, P * t : P * (t + 1)].bitcast(FP8X4),
                lhsT_scale=w2s[:, P * t : P * (t + 1)],
                rhs=hq[:].bitcast(FP8X4),
                rhs_scale=hs[:],
                start=True,
                stop=True,
            )

        def s2(c, t, whole):
            s = s2p.tile([P, 512], F32, name="s2")
            s2s[(c, t)] = s
            if whole:
                nc.scalar.activation(
                    out=s[:], in_=m2banks[(c, t)][:], func=ACT.Identity, bias=b2f[:, t : t + 1], scale=1.0
                )
            else:
                nc.scalar.activation(
                    out=s[:], in_=m2banks[(c, t)][:], func=ACT.Identity, bias=b2s[:, t : t + 1], scale=SLOPE
                )

        def st2(c, t, whole):
            h2 = h2p.tile([P, 512], F32, name="h2_%d_%d" % (t, c))
            h2s[(c, t)] = h2
            if whole:
                nc.vector.scalar_tensor_tensor(
                    out=h2[:], in0=s2s[(c, t)][:], scalar=SLOPE, in1=s2s[(c, t)][:], op0=ALU.mult, op1=ALU.max
                )
            else:
                nc.vector.scalar_tensor_tensor(
                    out=h2[:],
                    in0=m2banks[(c, t)][:],
                    scalar=b2f[:, t : t + 1],
                    in1=s2s[(c, t)][:],
                    op0=ALU.add,
                    op1=ALU.max,
                )

        def bn(c, t):
            nc.vector.bn_stats(out=stats[t][:, 6 * c : 6 * (c + 1)], in_=h2s[(c, t)][:])

        def agg(t):
            mv = const.tile([P, 2], F32, name="mv%d" % t)
            ve = const.tile([P, 1], F32, name="ve%d" % t)
            rstd = const.tile([P, 1], F32, name="rstd%d" % t)
            ca = const.tile([P, 1], F32, name="ca%d" % t)
            ma = const.tile([P, 1], F32, name="ma%d" % t)
            cb = const.tile([P, 1], F32, name="cb%d" % t)
            coefs[t] = (ca, cb)
            nc.vector.bn_aggr(out=mv[:], in_=stats[t][:])
            nc.gpsimd.tensor_scalar(out=ve[:], in0=mv[:, 1:2], scalar1=1.0, scalar2=EPS, op0=ALU.mult, op1=ALU.add)
            nc.gpsimd.tensor_tensor(out=rstd[:], in0=ve[:], in1=mhalf[:], op=ALU.pow)
            nc.gpsimd.tensor_tensor(out=ca[:], in0=rstd[:], in1=gaf[:, t : t + 1], op=ALU.mult)
            nc.gpsimd.tensor_tensor(out=ma[:], in0=mv[:, 0:1], in1=ca[:], op=ALU.mult)
            nc.gpsimd.tensor_tensor(out=cb[:], in0=bef[:, t : t + 1], in1=ma[:], op=ALU.subtract)

        def norm(c, t, eng):
            ca, cb = coefs[t]
            h2 = h2s[(c, t)]
            eng.tensor_scalar(out=h2[:], in0=h2[:], scalar1=ca[:, 0:1], scalar2=cb[:, 0:1], op0=ALU.mult, op1=ALU.add)

        def t_o(c, t):
            bank = pt.tile([P, 512], F32, name="ptb")
            obanks[(c, t)] = bank
            h2 = h2s[(c, t)]
            for i in range(RT):
                nc.tensor.transpose(bank[:, P * i : P * (i + 1)], h2[:, P * i : P * (i + 1)], ident[:])

        def ex(c, t):
            ost = ostp.tile([P, 512], F32, name="ost")
            if t == FT - 1 and c % 2 == 1:
                nc.vector.tensor_copy(out=ost[:], in_=obanks[(c, t)][:])
            else:
                nc.scalar.copy(out=ost[:], in_=obanks[(c, t)][:])
            nc.sync.dma_start(
                out=out_v[:, RT * c : RT * (c + 1), P * t : P * (t + 1)], in_=ost[:].rearrange("p (i f) -> p i f", i=RT)
            )

        units = [(c, t) for t in range(FT) for c in range(NCH)]
        pos = {"m": 0, "s": 0, "v": 0, "p": 0, "e": 0, "step": 0}
        agg_step = {}

        whole_of = {}

        def stats_of(c, t):
            bn(c, t)
            if c == NCH - 1:
                agg(t)
                agg_step[t] = pos["step"]
                for cc in range(NCH):
                    norm(cc, t, nc.gpsimd if t < FT - 1 else nc.vector)

        def v_units():
            while pos["v"] < pos["s"]:
                c, t = units[pos["v"]]
                st2(c, t, whole_of[(c, t)])
                if pos["v"] > 0:
                    stats_of(units[pos["v"] - 1][0], units[pos["v"] - 1][1])
                pos["v"] += 1
                if pos["v"] == len(units):
                    stats_of(c, t)

        t_x(0)
        xe(0)
        prep_w1()
        t_x(1)
        qx(0)
        xe(1)
        m1(0)
        t_x(2)
        bias1(0)
        qx(1)
        prep_w2()
        xe(2)
        for n in range(NCH):
            pos["step"] += 1
            if n + 1 < NCH:
                m1(n + 1)
            if n + 3 < NCH:
                t_x(n + 3)
            mu = []
            for j in range((1 if n >= 1 else 0) + EXTRA.get(n, 0)):
                if units[pos["m"]][0] <= n - 1:
                    mu.append(units[pos["m"]])
                    pos["m"] += 1
            for c, t in mu:
                m2(c, t)
            st1(n)
            v_units()
            qh(n)
            if n + 2 < NCH:
                qx(n + 2)
            if n + 1 < NCH:
                bias1(n + 1)
            if n + 3 < NCH:
                xe(n + 3)
            for c, t in mu:
                s2(c, t, True)
                whole_of[(c, t)] = True
                pos["s"] += 1
        while pos["v"] < len(units) or pos["e"] < len(units):
            pos["step"] += 1
            mu = units[pos["m"] : pos["m"] + GB]
            pos["m"] += len(mu)
            for c, t in mu:
                m2(c, t)
            pa = []
            for j in range(GB):
                if pos["p"] < len(units):
                    u = units[pos["p"]]
                    if u[1] in agg_step and pos["step"] - agg_step[u[1]] >= PLAG:
                        pa.append(u)
                        pos["p"] += 1
            for c, t in pa:
                t_o(c, t)
            v_units()
            for c, t in mu:
                s2(c, t, False)
                whole_of[(c, t)] = False
                pos["s"] += 1
            for c, t in pa:
                ex(c, t)
                pos["e"] += 1
